import numpy as np
import ml_dtypes


def mxq(x, axis, fmt="e4m3"):
    dtype, down = {"e4m3": (ml_dtypes.float8_e4m3fn, 7), "e5m2": (ml_dtypes.float8_e5m2, 14)}[fmt]
    v = np.moveaxis(np.asarray(x, np.float32).astype(ml_dtypes.bfloat16).astype(np.float64), axis, -1)
    blocks = v.reshape(v.shape[:-1] + (-1, 32))
    amax = np.abs(blocks).max(-1, keepdims=True)
    byte = np.maximum(np.where(amax > 0, np.frexp(amax)[1] - 1 + 127, 0) - down, 1)
    scale = np.exp2(byte - 127.0)
    codes = (blocks / scale).astype(np.float32).astype(dtype).astype(np.float64)
    return np.moveaxis((codes * scale).reshape(v.shape), -1, axis)


WIDE = False


def mx_kscale(k):
    if not WIDE:
        return np.ones(k)
    levels = np.array([10, -10, 5, -5, 0])
    a = np.random.permutation(np.resize(levels, k // 512 * 4)).reshape(k // 512, 4)
    idx = np.arange(k)
    return np.exp2(a[idx // 512, idx % 128 // 32])


BF16 = ml_dtypes.bfloat16


def bf(x):
    return np.asarray(x, np.float32).astype(BF16)


def f64(x):
    return np.asarray(x).astype(np.float64)


E2M1 = np.array([0.0, 0.5, 1.0, 1.5, 2.0, 3.0, 4.0, 6.0, -0.0, -0.5, -1.0, -1.5, -2.0, -3.0, -4.0, -6.0])


def pack_weight(w, fmt):
    k, n = w.shape
    w = f64(bf(w)).reshape(k // 32, 32, n)
    amax = np.abs(w).max(1)
    if fmt == "e4m3":
        byte = np.frexp(amax)[1] - 1 + 127 - 7
    else:
        mant, ex = np.frexp(amax / 6.0)
        byte = np.where(mant > 0.5, ex, ex - 1) + 127
    byte = np.clip(np.where(amax > 0, byte, 1), 1, 254)
    scaled = (w * np.exp2(127.0 - byte)[:, None, :]).reshape(k, n).astype(np.float32)
    by_word = np.ascontiguousarray(scaled.reshape(k // 512, 128, 4, n).transpose(0, 1, 3, 2))
    if fmt == "e4m3":
        words = by_word.astype(ml_dtypes.float8_e4m3fn).view(np.uint8)
    else:
        c = by_word.astype(ml_dtypes.float4_e2m1fn).view(np.uint8) & 0xF
        words = c[..., 0::2] | (c[..., 1::2] << 4)
    return np.ascontiguousarray(words), np.ascontiguousarray(byte.astype(np.uint8).reshape(k // 512, 16, n))


def unpack_weight(words, scales, fmt):
    g, p, n, _ = words.shape
    if fmt == "e4m3":
        vals = np.ascontiguousarray(words).view(ml_dtypes.float8_e4m3fn).astype(np.float64)
    else:
        nib = np.empty((g, p, n, 4), np.uint8)
        nib[..., 0::2] = words & 0xF
        nib[..., 1::2] = words >> 4
        vals = E2M1[nib]
    vals = vals * np.repeat(np.exp2(scales.astype(np.float64) - 127.0), 8, axis=1)[..., None]
    return vals.transpose(0, 1, 3, 2).reshape(g * 512, n)


B, S, HIDDEN, NUM_HEADS, HEAD_DIM = 2, 512, 1024, 16, 64
F = NUM_HEADS * HEAD_DIM
FMT = "e4m3"


def _split_heads(x):
    b, s, _ = x.shape
    return x.reshape(b, s, NUM_HEADS, HEAD_DIM).transpose(0, 2, 1, 3)


def setup_inputs():
    s = mx_kscale(HIDDEN)
    scale = 1.0 / np.sqrt(HIDDEN)
    hidden_states = bf(np.random.standard_normal((B, S, HIDDEN)) * s)
    Wq_words, Wq_scales = pack_weight(np.random.standard_normal((HIDDEN, F)) * scale / s[:, None], FMT)
    bq = bf(np.random.standard_normal(F) * 0.5)
    Wk_words, Wk_scales = pack_weight(np.random.standard_normal((HIDDEN, F)) * scale / s[:, None], FMT)
    bk = bf(np.random.standard_normal(F) * 0.5)
    Wv_words, Wv_scales = pack_weight(np.random.standard_normal((HIDDEN, F)) * scale / s[:, None], FMT)
    bv = bf(np.random.standard_normal(F) * 0.5)
    return {
        "hidden_states": hidden_states,
        "Wq_words": Wq_words,
        "Wq_scales": Wq_scales,
        "bq": bq,
        "Wk_words": Wk_words,
        "Wk_scales": Wk_scales,
        "bk": bk,
        "Wv_words": Wv_words,
        "Wv_scales": Wv_scales,
        "bv": bv,
    }


def reference(hidden_states, Wq_words, Wq_scales, bq, Wk_words, Wk_scales, bk, Wv_words, Wv_scales, bv):
    Wqkv = np.concatenate([
        unpack_weight(Wq_words, Wq_scales, FMT),
        unpack_weight(Wk_words, Wk_scales, FMT),
        unpack_weight(Wv_words, Wv_scales, FMT),
    ], axis=1)
    bqkv = np.concatenate([f64(bq), f64(bk), f64(bv)], axis=0)
    qkv = (mxq(f64(hidden_states), 2, "e4m3") @ Wqkv) + bqkv
    q, k, v = np.split(qkv, 3, axis=-1)
    return (_split_heads(q), _split_heads(k), _split_heads(v))

@@ -1,0 +1,182 @@
+from contextlib import ExitStack
+
+import concourse.mybir as mybir
+from concourse.masks import make_identity
+
+BF16 = mybir.dt.bfloat16
+F32 = mybir.dt.float32
+I32 = mybir.dt.int32
+U8 = mybir.dt.uint8
+FP8X4 = mybir.dt.float8_e4m3fn_x4
+ADD = mybir.AluOpType.add
+
+P = 128
+PACK = 4
+K_PASS = P * PACK
+BATCH, SEQ, HIDDEN = 2, 512, 1024
+HEADS, HEAD_DIM = 16, 64
+FEATURES = HEADS * HEAD_DIM
+WEIGHTS = 3
+PASSES = HIDDEN // K_PASS
+TOKEN_TILES = BATCH * SEQ // P
+BANK = 512
+TILE_WIDTHS = [BANK // 2] * 2 + [BANK] * (WEIGHTS * FEATURES // BANK - 2) + [BANK // 2] * 2
+PAIRS = 2
+HALVES = 2
+X_LOADS = 4
+QUADRANTS = 4
+SCALE_ROWS = 4
+
+FLOPS = 2 * BATCH * SEQ * HIDDEN * WEIGHTS * FEATURES
+
+
+def tile_attention_before_kernel(
+    tc,
+    hidden_states,
+    Wq_words,
+    Wq_scales,
+    bq,
+    Wk_words,
+    Wk_scales,
+    bk,
+    Wv_words,
+    Wv_scales,
+    bv,
+    out_0,
+    out_1,
+    out_2,
+):
+    nc = tc.nc
+    weight_words = [Wq_words, Wk_words, Wv_words]
+    weight_scales = [Wq_scales, Wk_scales, Wv_scales]
+    biases = [bq, bk, bv]
+    outs = [out_0, out_1, out_2]
+
+    with ExitStack() as ctx:
+        keep = ctx.enter_context(tc.tile_pool(name="keep", bufs=1))
+        psum = ctx.enter_context(tc.psum_pool(name="psum", bufs=8))
+
+        x_sb = keep.tile([P, TOKEN_TILES, HIDDEN], BF16)
+        x_grouped = keep.tile([P, TOKEN_TILES, PASSES * P * PACK], BF16, align_bytes=64)
+        x_codes = keep.tile([P, TOKEN_TILES, PASSES * P], I32, align_bytes=64)
+        x_planes = keep.tile([P, TOKEN_TILES, PASSES * P], U8, align_bytes=64)
+        w_codes = keep.tile([P, WEIGHTS, HALVES, PASSES, FEATURES // HALVES], I32, align_bytes=64)
+        w_planes = [
+            keep.tile([P, FEATURES], U8, align_bytes=64, name="w_planes%d" % w) for w in range(WEIGHTS)
+        ]
+        identity = keep.tile([P, P], F32)
+        ones = keep.tile([P, P], BF16)
+        bias_rows = keep.tile([P, WEIGHTS * FEATURES], BF16)
+        bias_all = keep.tile([P, WEIGHTS * FEATURES], F32)
+        staged = keep.tile([P, WEIGHTS * HEADS, TOKEN_TILES, HEAD_DIM], F32)
+
+        nc.vector.memset(bias_rows[:].bitcast(I32), 0)
+        for w in range(WEIGHTS):
+            nc.vector.memset(w_planes[w][:].bitcast(I32), 0)
+        nc.vector.memset(ones[:], 1.0)
+        make_identity(nc, identity[:])
+
+        def load_scales(w):
+            for quadrant in range(QUADRANTS):
+                top = 32 * quadrant
+                rows = weight_scales[w][:, SCALE_ROWS * quadrant : SCALE_ROWS * (quadrant + 1), :]
+                nc.sync.dma_start(
+                    out=w_planes[w][top : top + PASSES * SCALE_ROWS, :].bitcast(I32),
+                    in_=rows.bitcast(I32),
+                )
+
+        def load_codes(w, half):
+            cols = slice(FEATURES // HALVES * half, FEATURES // HALVES * (half + 1))
+            nc.sync.dma_start(
+                out=w_codes[:, w, half, :, :],
+                in_=weight_words[w][:, :, cols, :].rearrange("g p n t -> p g (n t)").bitcast(I32),
+            )
+
+        x_rows = hidden_states.rearrange("b (u j) k -> u b (j k)", j=TOKEN_TILES)
+        x_flat = x_sb[:].rearrange("p j k -> p (j k)")
+        piece = TOKEN_TILES * HIDDEN // X_LOADS
+        for i in range(X_LOADS):
+            nc.sync.dma_start(
+                out=x_flat[:, piece * i : piece * (i + 1)],
+                in_=x_rows[:, :, piece * i : piece * (i + 1)],
+            )
+            if i == 0:
+                for w in range(WEIGHTS):
+                    nc.sync.dma_start(
+                        out=bias_rows[0:1, FEATURES * w : FEATURES * (w + 1)],
+                        in_=biases[w].rearrange("(o n) -> o n", o=1),
+                    )
+        for w in range(WEIGHTS):
+            load_codes(w, 0)
+            load_scales(w)
+            load_codes(w, 1)
+
+        words_per_pass = K_PASS // 2
+        for j in range(TOKEN_TILES):
+            x_words = x_sb[:, j, :].bitcast(F32)
+            flipped = psum.tile([P, PASSES, PAIRS, P], F32, tag="bank")
+            for g in range(PASSES):
+                for e in range(PAIRS):
+                    nc.tensor.transpose(
+                        flipped[:, g, e, :],
+                        x_words[:, words_per_pass * g + e : words_per_pass * (g + 1) : PAIRS],
+                        identity[:],
+                    )
+            nc.scalar.copy(
+                out=x_grouped[:, j, :].bitcast(F32).rearrange("p (g m e) -> p g m e", g=PASSES, e=PAIRS),
+                in_=flipped[:].rearrange("p g e m -> p g m e"),
+            )
+            nc.vector.quantize_mx(
+                out=x_codes[:, j, :].bitcast(FP8X4),
+                scales=x_planes[:, j, :],
+                in_=x_grouped[:, j, :],
+            )
+
+        def broadcast_bias(first, width):
+            cols = slice(first, first + width)
+            bias_bank = psum.tile([P, width], F32, tag="bank")
+            nc.tensor.matmul(bias_bank[:], lhsT=ones[:], rhs=bias_rows[:, cols], start=True, stop=True)
+            nc.scalar.copy(out=bias_all[:, cols], in_=bias_bank[:])
+
+        out_rows = [o.rearrange("b h (u j) d -> h u b (j d)", j=TOKEN_TILES) for o in outs]
+        tile_starts = [sum(TILE_WIDTHS[:c]) for c in range(len(TILE_WIDTHS))]
+        broadcast_bias(tile_starts[0], TILE_WIDTHS[0])
+        for c, (first, width) in enumerate(zip(tile_starts, TILE_WIDTHS)):
+            if c + 1 < len(TILE_WIDTHS):
+                broadcast_bias(tile_starts[c + 1], TILE_WIDTHS[c + 1])
+            w = first // FEATURES
+            cols = slice(first % FEATURES, first % FEATURES + width)
+            half = (first % FEATURES) // (FEATURES // HALVES)
+            cols_in_half = slice(first % (FEATURES // HALVES), first % (FEATURES // HALVES) + width)
+            first_head = first // HEAD_DIM
+            heads_in_tile = width // HEAD_DIM
+            heads = slice(first_head, first_head + heads_in_tile)
+            bias_heads = bias_all[:, first : first + width].rearrange("p (h d) -> p h d", d=HEAD_DIM)
+            for j in range(TOKEN_TILES):
+                acc = psum.tile([P, width], F32, tag="bank")
+                for g in range(PASSES):
+                    tokens = slice(P * g, P * (g + 1))
+                    nc.tensor.matmul_mx(
+                        out=acc[:],
+                        lhsT=x_codes[:, j, tokens].bitcast(FP8X4),
+                        lhsT_scale=x_planes[:, j, tokens],
+                        rhs=w_codes[:, w, half, g, cols_in_half].bitcast(FP8X4),
+                        rhs_scale=w_planes[w][SCALE_ROWS * g : P, cols],
+                        start=(g == 0),
+                        stop=(g == PASSES - 1),
+                    )
+                acc_heads = acc[:].rearrange("p (h d) -> p h d", d=HEAD_DIM)
+                if j % 3 == 0:
+                    nc.scalar.copy(out=staged[:, heads, j, :], in_=acc_heads)
+                    nc.gpsimd.tensor_tensor(
+                        out=staged[:, heads, j, :], in0=staged[:, heads, j, :], in1=bias_heads, op=ADD
+                    )
+                else:
+                    nc.vector.tensor_tensor(
+                        out=staged[:, heads, j, :], in0=acc_heads, in1=bias_heads, op=ADD
+                    )
+            for head in range(first_head, first_head + heads_in_tile):
+                nc.sync.dma_start(
+                    out=out_rows[w][head % HEADS],
+                    in_=staged[:, head, :, :].rearrange("p j d -> p (j d)"),
+                )

@@ -22,7 +22,6 @@ TOKEN_TILES = BATCH * SEQ // P
 BANK = 512
 TILE_WIDTHS = [BANK // 2] * 2 + [BANK] * (WEIGHTS * FEATURES // BANK - 2) + [BANK // 2] * 2
 PAIRS = 2
-HALVES = 2
 X_LOADS = 4
 QUADRANTS = 4
 SCALE_ROWS = 4
@@ -60,7 +59,7 @@ def tile_attention_before_kernel(
         x_grouped = keep.tile([P, TOKEN_TILES, PASSES * P * PACK], BF16, align_bytes=64)
         x_codes = keep.tile([P, TOKEN_TILES, PASSES * P], I32, align_bytes=64)
         x_planes = keep.tile([P, TOKEN_TILES, PASSES * P], U8, align_bytes=64)
-        w_codes = keep.tile([P, WEIGHTS, HALVES, PASSES, FEATURES // HALVES], I32, align_bytes=64)
+        w_codes = keep.tile([P, WEIGHTS, PASSES, FEATURES], I32, align_bytes=64)
         w_planes = [
             keep.tile([P, FEATURES], U8, align_bytes=64, name="w_planes%d" % w) for w in range(WEIGHTS)
         ]
@@ -80,16 +79,15 @@ def tile_attention_before_kernel(
             for quadrant in range(QUADRANTS):
                 top = 32 * quadrant
                 rows = weight_scales[w][:, SCALE_ROWS * quadrant : SCALE_ROWS * (quadrant + 1), :]
-                nc.sync.dma_start(
-                    out=w_planes[w][top : top + PASSES * SCALE_ROWS, :].bitcast(I32),
-                    in_=rows.bitcast(I32),
+                nc.gpsimd.dma_start(
+                    out=w_planes[w][top : top + PASSES * SCALE_ROWS, :].bitcast(F32),
+                    in_=rows.bitcast(F32),
                 )
 
-        def load_codes(w, half):
-            cols = slice(FEATURES // HALVES * half, FEATURES // HALVES * (half + 1))
+        def load_codes(w):
             nc.sync.dma_start(
-                out=w_codes[:, w, half, :, :],
-                in_=weight_words[w][:, :, cols, :].rearrange("g p n t -> p g (n t)").bitcast(I32),
+                out=w_codes[:, w, :, :],
+                in_=weight_words[w].rearrange("g p n t -> p g (n t)").bitcast(I32),
             )
 
         x_rows = hidden_states.rearrange("b (u j) k -> u b (j k)", j=TOKEN_TILES)
@@ -107,9 +105,8 @@ def tile_attention_before_kernel(
                         in_=biases[w].rearrange("(o n) -> o n", o=1),
                     )
         for w in range(WEIGHTS):
-            load_codes(w, 0)
+            load_codes(w)
             load_scales(w)
-            load_codes(w, 1)
 
         words_per_pass = K_PASS // 2
         for j in range(TOKEN_TILES):
@@ -146,8 +143,6 @@ def tile_attention_before_kernel(
                 broadcast_bias(tile_starts[c + 1], TILE_WIDTHS[c + 1])
             w = first // FEATURES
             cols = slice(first % FEATURES, first % FEATURES + width)
-            half = (first % FEATURES) // (FEATURES // HALVES)
-            cols_in_half = slice(first % (FEATURES // HALVES), first % (FEATURES // HALVES) + width)
             first_head = first // HEAD_DIM
             heads_in_tile = width // HEAD_DIM
             heads = slice(first_head, first_head + heads_in_tile)
@@ -160,7 +155,7 @@ def tile_attention_before_kernel(
                         out=acc[:],
                         lhsT=x_codes[:, j, tokens].bitcast(FP8X4),
                         lhsT_scale=x_planes[:, j, tokens],
-                        rhs=w_codes[:, w, half, g, cols_in_half].bitcast(FP8X4),
+                        rhs=w_codes[:, w, g, cols].bitcast(FP8X4),
                         rhs_scale=w_planes[w][SCALE_ROWS * g : P, cols],
                         start=(g == 0),
                         stop=(g == PASSES - 1),

@@ -20,9 +20,14 @@ WEIGHTS = 3
 PASSES = HIDDEN // K_PASS
 TOKEN_TILES = BATCH * SEQ // P
 BANK = 512
-TILE_WIDTHS = [BANK // 2] * 2 + [BANK] * (WEIGHTS * FEATURES // BANK - 2) + [BANK // 2] * 2
+N_TILE = 256
+COLUMN_TILES = WEIGHTS * FEATURES // N_TILE
+HEADS_PER_TILE = N_TILE // HEAD_DIM
+TOKEN_TILES_PER_BANK = BANK // N_TILE
+BANKS_PER_TILE = TOKEN_TILES // TOKEN_TILES_PER_BANK
 PAIRS = 2
-X_LOADS = 4
+HALVES = 2
+X_PIECES = [1, 1, 2, 2, 2]
 QUADRANTS = 4
 SCALE_ROWS = 4
 
@@ -59,9 +64,10 @@ def tile_attention_before_kernel(
         x_grouped = keep.tile([P, TOKEN_TILES, PASSES * P * PACK], BF16, align_bytes=64)
         x_codes = keep.tile([P, TOKEN_TILES, PASSES * P], I32, align_bytes=64)
         x_planes = keep.tile([P, TOKEN_TILES, PASSES * P], U8, align_bytes=64)
-        w_codes = keep.tile([P, WEIGHTS, PASSES, FEATURES], I32, align_bytes=64)
+        w_codes = keep.tile([P, WEIGHTS, HALVES, PASSES, FEATURES // HALVES], I32, align_bytes=64)
         w_planes = [
-            keep.tile([P, FEATURES], U8, align_bytes=64, name="w_planes%d" % w) for w in range(WEIGHTS)
+            keep.tile([P, PASSES, FEATURES], U8, align_bytes=64, name="w_planes%d" % w)
+            for w in range(WEIGHTS)
         ]
         identity = keep.tile([P, P], F32)
         ones = keep.tile([P, P], BF16)
@@ -71,7 +77,7 @@ def tile_attention_before_kernel(
 
         nc.vector.memset(bias_rows[:].bitcast(I32), 0)
         for w in range(WEIGHTS):
-            nc.vector.memset(w_planes[w][:].bitcast(I32), 0)
+            nc.vector.memset(w_planes[w][:].rearrange("p g n -> p (g n)").bitcast(I32), 0)
         nc.vector.memset(ones[:], 1.0)
         make_identity(nc, identity[:])
 
@@ -79,25 +85,23 @@ def tile_attention_before_kernel(
             for quadrant in range(QUADRANTS):
                 top = 32 * quadrant
                 rows = weight_scales[w][:, SCALE_ROWS * quadrant : SCALE_ROWS * (quadrant + 1), :]
-                nc.gpsimd.dma_start(
-                    out=w_planes[w][top : top + PASSES * SCALE_ROWS, :].bitcast(F32),
-                    in_=rows.bitcast(F32),
+                nc.sync.dma_start(
+                    out=w_planes[w][top : top + SCALE_ROWS, :, :].bitcast(I32),
+                    in_=rows.rearrange("g r n -> r g n").bitcast(I32),
                 )
 
-        def load_codes(w):
+        def load_codes(w, half):
+            cols = slice(FEATURES // HALVES * half, FEATURES // HALVES * (half + 1))
             nc.sync.dma_start(
-                out=w_codes[:, w, :, :],
-                in_=weight_words[w].rearrange("g p n t -> p g (n t)").bitcast(I32),
+                out=w_codes[:, w, half, :, :],
+                in_=weight_words[w][:, :, cols, :].rearrange("g p n t -> p g (n t)").bitcast(I32),
             )
 
         x_rows = hidden_states.rearrange("b (u j) k -> u b (j k)", j=TOKEN_TILES)
         x_flat = x_sb[:].rearrange("p j k -> p (j k)")
-        piece = TOKEN_TILES * HIDDEN // X_LOADS
-        for i in range(X_LOADS):
-            nc.sync.dma_start(
-                out=x_flat[:, piece * i : piece * (i + 1)],
-                in_=x_rows[:, :, piece * i : piece * (i + 1)],
-            )
+        for i in range(len(X_PIECES)):
+            piece = slice(HIDDEN * sum(X_PIECES[:i]), HIDDEN * sum(X_PIECES[: i + 1]))
+            nc.sync.dma_start(out=x_flat[:, piece], in_=x_rows[:, :, piece])
             if i == 0:
                 for w in range(WEIGHTS):
                     nc.sync.dma_start(
@@ -105,8 +109,9 @@ def tile_attention_before_kernel(
                         in_=biases[w].rearrange("(o n) -> o n", o=1),
                     )
         for w in range(WEIGHTS):
-            load_codes(w)
+            load_codes(w, 0)
             load_scales(w)
+            load_codes(w, 1)
 
         words_per_pass = K_PASS // 2
         for j in range(TOKEN_TILES):
@@ -129,48 +134,52 @@ def tile_attention_before_kernel(
                 in_=x_grouped[:, j, :],
             )
 
-        def broadcast_bias(first, width):
-            cols = slice(first, first + width)
-            bias_bank = psum.tile([P, width], F32, tag="bank")
+        def broadcast_bias(c):
+            cols = slice(N_TILE * c, N_TILE * (c + 1))
+            bias_bank = psum.tile([P, N_TILE], F32, tag="bank")
             nc.tensor.matmul(bias_bank[:], lhsT=ones[:], rhs=bias_rows[:, cols], start=True, stop=True)
             nc.scalar.copy(out=bias_all[:, cols], in_=bias_bank[:])
 
         out_rows = [o.rearrange("b h (u j) d -> h u b (j d)", j=TOKEN_TILES) for o in outs]
-        tile_starts = [sum(TILE_WIDTHS[:c]) for c in range(len(TILE_WIDTHS))]
-        broadcast_bias(tile_starts[0], TILE_WIDTHS[0])
-        for c, (first, width) in enumerate(zip(tile_starts, TILE_WIDTHS)):
-            if c + 1 < len(TILE_WIDTHS):
-                broadcast_bias(tile_starts[c + 1], TILE_WIDTHS[c + 1])
-            w = first // FEATURES
-            cols = slice(first % FEATURES, first % FEATURES + width)
-            first_head = first // HEAD_DIM
-            heads_in_tile = width // HEAD_DIM
-            heads = slice(first_head, first_head + heads_in_tile)
-            bias_heads = bias_all[:, first : first + width].rearrange("p (h d) -> p h d", d=HEAD_DIM)
-            for j in range(TOKEN_TILES):
-                acc = psum.tile([P, width], F32, tag="bank")
-                for g in range(PASSES):
-                    tokens = slice(P * g, P * (g + 1))
-                    nc.tensor.matmul_mx(
-                        out=acc[:],
-                        lhsT=x_codes[:, j, tokens].bitcast(FP8X4),
-                        lhsT_scale=x_planes[:, j, tokens],
-                        rhs=w_codes[:, w, g, cols].bitcast(FP8X4),
-                        rhs_scale=w_planes[w][SCALE_ROWS * g : P, cols],
-                        start=(g == 0),
-                        stop=(g == PASSES - 1),
-                    )
-                acc_heads = acc[:].rearrange("p (h d) -> p h d", d=HEAD_DIM)
-                if j % 3 == 0:
-                    nc.scalar.copy(out=staged[:, heads, j, :], in_=acc_heads)
-                    nc.gpsimd.tensor_tensor(
-                        out=staged[:, heads, j, :], in0=staged[:, heads, j, :], in1=bias_heads, op=ADD
-                    )
+        tiles_per_half = FEATURES // HALVES // N_TILE
+        broadcast_bias(0)
+        for c in range(COLUMN_TILES):
+            if c + 1 < COLUMN_TILES:
+                broadcast_bias(c + 1)
+            w = c // (HALVES * tiles_per_half)
+            half = c // tiles_per_half % HALVES
+            cols_in_half = slice(N_TILE * (c % tiles_per_half), N_TILE * (c % tiles_per_half + 1))
+            cols_in_weight = slice(N_TILE * c % FEATURES, N_TILE * c % FEATURES + N_TILE)
+            heads = slice(HEADS_PER_TILE * c, HEADS_PER_TILE * (c + 1))
+            bias_heads = (
+                bias_all[:, N_TILE * c : N_TILE * (c + 1)]
+                .rearrange("p (i h d) -> p i h d", i=1, d=HEAD_DIM)
+                .to_broadcast([P, TOKEN_TILES_PER_BANK, HEADS_PER_TILE, HEAD_DIM])
+            )
+            for bank in range(BANKS_PER_TILE):
+                acc = psum.tile([P, TOKEN_TILES_PER_BANK, N_TILE], F32, tag="bank")
+                for i in range(TOKEN_TILES_PER_BANK):
+                    j = TOKEN_TILES_PER_BANK * bank + i
+                    for g in range(PASSES):
+                        tokens = slice(P * g, P * (g + 1))
+                        nc.tensor.matmul_mx(
+                            out=acc[:, i, :],
+                            lhsT=x_codes[:, j, tokens].bitcast(FP8X4),
+                            lhsT_scale=x_planes[:, j, tokens],
+                            rhs=w_codes[:, w, half, g, cols_in_half].bitcast(FP8X4),
+                            rhs_scale=w_planes[w][:, g, cols_in_weight],
+                            start=(g == 0),
+                            stop=(g == PASSES - 1),
+                        )
+                acc_heads = acc[:].rearrange("p i (h d) -> p i h d", d=HEAD_DIM)
+                token_tiles = slice(TOKEN_TILES_PER_BANK * bank, TOKEN_TILES_PER_BANK * (bank + 1))
+                landing = staged[:, heads, token_tiles, :].rearrange("p h i d -> p i h d")
+                if (BANKS_PER_TILE * c + bank) % 3 == 0:
+                    nc.scalar.copy(out=landing, in_=acc_heads)
+                    nc.gpsimd.tensor_tensor(out=landing, in0=landing, in1=bias_heads, op=ADD)
                 else:
-                    nc.vector.tensor_tensor(
-                        out=staged[:, heads, j, :], in0=acc_heads, in1=bias_heads, op=ADD
-                    )
-            for head in range(first_head, first_head + heads_in_tile):
+                    nc.vector.tensor_tensor(out=landing, in0=acc_heads, in1=bias_heads, op=ADD)
+            for head in range(HEADS_PER_TILE * c, HEADS_PER_TILE * (c + 1)):
                 nc.sync.dma_start(
                     out=out_rows[w][head % HEADS],
                     in_=staged[:, head, :, :].rearrange("p j d -> p (j d)"),

@@ -140,7 +140,7 @@ def tile_attention_before_kernel(
             nc.tensor.matmul(bias_bank[:], lhsT=ones[:], rhs=bias_rows[:, cols], start=True, stop=True)
             nc.scalar.copy(out=bias_all[:, cols], in_=bias_bank[:])
 
-        out_rows = [o.rearrange("b h (u j) d -> h u b (j d)", j=TOKEN_TILES) for o in outs]
+        out_rows = [o.rearrange("b h (u j) d -> b u h (j d)", j=TOKEN_TILES) for o in outs]
         tiles_per_half = FEATURES // HALVES // N_TILE
         broadcast_bias(0)
         for c in range(COLUMN_TILES):
@@ -179,8 +179,9 @@ def tile_attention_before_kernel(
                     nc.gpsimd.tensor_tensor(out=landing, in0=landing, in1=bias_heads, op=ADD)
                 else:
                     nc.vector.tensor_tensor(out=landing, in0=acc_heads, in1=bias_heads, op=ADD)
-            for head in range(HEADS_PER_TILE * c, HEADS_PER_TILE * (c + 1)):
+            first_head = HEADS_PER_TILE * c % HEADS
+            for b in range(BATCH):
                 nc.sync.dma_start(
-                    out=out_rows[w][head % HEADS],
-                    in_=staged[:, head, :, :].rearrange("p j d -> p (j d)"),
+                    out=out_rows[w][b][:, first_head : first_head + HEADS_PER_TILE, :],
+                    in_=staged[b:P:BATCH, heads, :, :].rearrange("p h j d -> p h (j d)"),
                 )

@@ -28,6 +28,7 @@ BANKS_PER_TILE = TOKEN_TILES // TOKEN_TILES_PER_BANK
 PAIRS = 2
 HALVES = 2
 X_PIECES = [1, 1, 2, 2, 2]
+WARM_UP = 4
 QUADRANTS = 4
 SCALE_ROWS = 4
 
@@ -70,16 +71,20 @@ def tile_attention_before_kernel(
             for w in range(WEIGHTS)
         ]
         identity = keep.tile([P, P], F32)
-        ones = keep.tile([P, P], BF16)
+        ones = keep.tile([P, BANK], BF16)
         bias_rows = keep.tile([P, WEIGHTS * FEATURES], BF16)
-        bias_all = keep.tile([P, WEIGHTS * FEATURES], F32)
+        bias_all = keep.tile([P, WEIGHTS * FEATURES], BF16)
         staged = keep.tile([P, WEIGHTS * HEADS, TOKEN_TILES, HEAD_DIM], F32)
 
+        nc.vector.memset(ones[:], 1.0)
         nc.vector.memset(bias_rows[:].bitcast(I32), 0)
         for w in range(WEIGHTS):
             nc.vector.memset(w_planes[w][:].rearrange("p g n -> p (g n)").bitcast(I32), 0)
-        nc.vector.memset(ones[:], 1.0)
         make_identity(nc, identity[:])
+
+        warm_bank = psum.tile([P, BANK], F32, tag="bank")
+        for i in range(WARM_UP):
+            nc.tensor.matmul(warm_bank[:], lhsT=ones[:, 0:P], rhs=ones[:], start=True, stop=True)
 
         def load_scales(w):
             for quadrant in range(QUADRANTS):
@@ -114,6 +119,7 @@ def tile_attention_before_kernel(
             load_codes(w, 1)
 
         words_per_pass = K_PASS // 2
+        bias_banks = {}
         for j in range(TOKEN_TILES):
             x_words = x_sb[:, j, :].bitcast(F32)
             flipped = psum.tile([P, PASSES, PAIRS, P], F32, tag="bank")
@@ -133,19 +139,25 @@ def tile_attention_before_kernel(
                 scales=x_planes[:, j, :],
                 in_=x_grouped[:, j, :],
             )
-
-        def broadcast_bias(c):
-            cols = slice(N_TILE * c, N_TILE * (c + 1))
-            bias_bank = psum.tile([P, N_TILE], F32, tag="bank")
-            nc.tensor.matmul(bias_bank[:], lhsT=ones[:], rhs=bias_rows[:, cols], start=True, stop=True)
-            nc.scalar.copy(out=bias_all[:, cols], in_=bias_bank[:])
+            if 1 <= j <= WEIGHTS * HALVES:
+                w, half = divmod(j - 1, HALVES)
+                if half == 0:
+                    bias_banks[w] = psum.tile([P, FEATURES], BF16, tag="bank", name="bias_bank%d" % w)
+                nc.tensor.matmul(
+                    bias_banks[w][:, BANK * half : BANK * (half + 1)],
+                    lhsT=ones[:, 0:P],
+                    rhs=bias_rows[:, FEATURES * w + BANK * half : FEATURES * w + BANK * (half + 1)],
+                    start=True,
+                    stop=True,
+                )
+                if half == HALVES - 1:
+                    nc.vector.tensor_copy(
+                        out=bias_all[:, FEATURES * w : FEATURES * (w + 1)], in_=bias_banks[w][:]
+                    )
 
         out_rows = [o.rearrange("b h (u j) d -> b u h (j d)", j=TOKEN_TILES) for o in outs]
         tiles_per_half = FEATURES // HALVES // N_TILE
-        broadcast_bias(0)
         for c in range(COLUMN_TILES):
-            if c + 1 < COLUMN_TILES:
-                broadcast_bias(c + 1)
             w = c // (HALVES * tiles_per_half)
             half = c // tiles_per_half % HALVES
             cols_in_half = slice(N_TILE * (c % tiles_per_half), N_TILE * (c % tiles_per_half + 1))

@@ -186,7 +186,7 @@ def tile_attention_before_kernel(
                 acc_heads = acc[:].rearrange("p i (h d) -> p i h d", d=HEAD_DIM)
                 token_tiles = slice(TOKEN_TILES_PER_BANK * bank, TOKEN_TILES_PER_BANK * (bank + 1))
                 landing = staged[:, heads, token_tiles, :].rearrange("p h i d -> p i h d")
-                if (BANKS_PER_TILE * c + bank) % 3 == 0:
+                if (BANKS_PER_TILE * c + bank) % 5 == 0:
                     nc.scalar.copy(out=landing, in_=acc_heads)
                     nc.gpsimd.tensor_tensor(out=landing, in0=landing, in1=bias_heads, op=ADD)
                 else:

@@ -21,10 +21,7 @@ PASSES = HIDDEN // K_PASS
 TOKEN_TILES = BATCH * SEQ // P
 BANK = 512
 N_TILE = 256
-COLUMN_TILES = WEIGHTS * FEATURES // N_TILE
-HEADS_PER_TILE = N_TILE // HEAD_DIM
-TOKEN_TILES_PER_BANK = BANK // N_TILE
-BANKS_PER_TILE = TOKEN_TILES // TOKEN_TILES_PER_BANK
+COLUMN_TILES = [N_TILE] * (WEIGHTS * FEATURES // N_TILE - 1) + [N_TILE // 2] * 2
 PAIRS = 2
 HALVES = 2
 X_PIECES = [1, 1, 2, 2, 2]
@@ -87,12 +84,11 @@ def tile_attention_before_kernel(
             nc.tensor.matmul(warm_bank[:], lhsT=ones[:, 0:P], rhs=ones[:], start=True, stop=True)
 
         def load_scales(w):
-            for quadrant in range(QUADRANTS):
-                top = 32 * quadrant
-                rows = weight_scales[w][:, SCALE_ROWS * quadrant : SCALE_ROWS * (quadrant + 1), :]
+            rows = weight_scales[w].rearrange("g (q r) n -> r q g n", r=SCALE_ROWS)
+            for r in range(SCALE_ROWS):
                 nc.sync.dma_start(
-                    out=w_planes[w][top : top + SCALE_ROWS, :, :].bitcast(I32),
-                    in_=rows.rearrange("g r n -> r g n").bitcast(I32),
+                    out=w_planes[w][r : P : P // QUADRANTS, :, :].bitcast(I32),
+                    in_=rows[r].bitcast(I32),
                 )
 
         def load_codes(w, half):
@@ -156,44 +152,49 @@ def tile_attention_before_kernel(
                     )
 
         out_rows = [o.rearrange("b h (u j) d -> b u h (j d)", j=TOKEN_TILES) for o in outs]
-        tiles_per_half = FEATURES // HALVES // N_TILE
-        for c in range(COLUMN_TILES):
-            w = c // (HALVES * tiles_per_half)
-            half = c // tiles_per_half % HALVES
-            cols_in_half = slice(N_TILE * (c % tiles_per_half), N_TILE * (c % tiles_per_half + 1))
-            cols_in_weight = slice(N_TILE * c % FEATURES, N_TILE * c % FEATURES + N_TILE)
-            heads = slice(HEADS_PER_TILE * c, HEADS_PER_TILE * (c + 1))
+        first = 0
+        banks_done = 0
+        for width in COLUMN_TILES:
+            w = first // FEATURES
+            in_weight = first % FEATURES
+            half = in_weight // (FEATURES // HALVES)
+            in_half = in_weight % (FEATURES // HALVES)
+            heads_here = width // HEAD_DIM
+            heads = slice(first // HEAD_DIM, first // HEAD_DIM + heads_here)
+            per_bank = BANK // width
             bias_heads = (
-                bias_all[:, N_TILE * c : N_TILE * (c + 1)]
+                bias_all[:, first : first + width]
                 .rearrange("p (i h d) -> p i h d", i=1, d=HEAD_DIM)
-                .to_broadcast([P, TOKEN_TILES_PER_BANK, HEADS_PER_TILE, HEAD_DIM])
+                .to_broadcast([P, per_bank, heads_here, HEAD_DIM])
             )
-            for bank in range(BANKS_PER_TILE):
-                acc = psum.tile([P, TOKEN_TILES_PER_BANK, N_TILE], F32, tag="bank")
-                for i in range(TOKEN_TILES_PER_BANK):
-                    j = TOKEN_TILES_PER_BANK * bank + i
+            for bank in range(TOKEN_TILES // per_bank):
+                acc = psum.tile([P, per_bank, width], F32, tag="bank")
+                for i in range(per_bank):
+                    j = per_bank * bank + i
                     for g in range(PASSES):
                         tokens = slice(P * g, P * (g + 1))
                         nc.tensor.matmul_mx(
                             out=acc[:, i, :],
                             lhsT=x_codes[:, j, tokens].bitcast(FP8X4),
                             lhsT_scale=x_planes[:, j, tokens],
-                            rhs=w_codes[:, w, half, g, cols_in_half].bitcast(FP8X4),
-                            rhs_scale=w_planes[w][:, g, cols_in_weight],
+                            rhs=w_codes[:, w, half, g, in_half : in_half + width].bitcast(FP8X4),
+                            rhs_scale=w_planes[w][:, g, in_weight : in_weight + width],
                             start=(g == 0),
                             stop=(g == PASSES - 1),
                         )
                 acc_heads = acc[:].rearrange("p i (h d) -> p i h d", d=HEAD_DIM)
-                token_tiles = slice(TOKEN_TILES_PER_BANK * bank, TOKEN_TILES_PER_BANK * (bank + 1))
+                token_tiles = slice(per_bank * bank, per_bank * (bank + 1))
                 landing = staged[:, heads, token_tiles, :].rearrange("p h i d -> p i h d")
-                if (BANKS_PER_TILE * c + bank) % 5 == 0:
+                if width == N_TILE and banks_done % 5 == 0:
                     nc.scalar.copy(out=landing, in_=acc_heads)
                     nc.gpsimd.tensor_tensor(out=landing, in0=landing, in1=bias_heads, op=ADD)
                 else:
                     nc.vector.tensor_tensor(out=landing, in0=acc_heads, in1=bias_heads, op=ADD)
-            first_head = HEADS_PER_TILE * c % HEADS
+                banks_done += 1
+            first_head = in_weight // HEAD_DIM
             for b in range(BATCH):
                 nc.sync.dma_start(
-                    out=out_rows[w][b][:, first_head : first_head + HEADS_PER_TILE, :],
+                    out=out_rows[w][b][:, first_head : first_head + heads_here, :],
                     in_=staged[b:P:BATCH, heads, :, :].rearrange("p h j d -> p h (j d)"),
                 )
+            first += width

@@ -25,6 +25,7 @@ COLUMN_TILES = [N_TILE] * (WEIGHTS * FEATURES // N_TILE - 1) + [N_TILE // 2] * 2
 PAIRS = 2
 HALVES = 2
 X_PIECES = [1, 1, 2, 2, 2]
+BIAS_SLOTS = {1: [(0, 0), (0, 1)], 3: [(1, 0)], 4: [(1, 1)], 5: [(2, 0)], 6: [(2, 1)]}
 WARM_UP = 4
 QUADRANTS = 4
 SCALE_ROWS = 4
@@ -74,7 +75,8 @@ def tile_attention_before_kernel(
         staged = keep.tile([P, WEIGHTS * HEADS, TOKEN_TILES, HEAD_DIM], F32)
 
         nc.vector.memset(ones[:], 1.0)
-        nc.vector.memset(bias_rows[:].bitcast(I32), 0)
+        for w in range(WEIGHTS):
+            nc.vector.memset(bias_rows[:, FEATURES * w : FEATURES * (w + 1)].bitcast(I32), 0)
         for w in range(WEIGHTS):
             nc.vector.memset(w_planes[w][:].rearrange("p g n -> p (g n)").bitcast(I32), 0)
         make_identity(nc, identity[:])
@@ -91,11 +93,17 @@ def tile_attention_before_kernel(
                     in_=rows[r].bitcast(I32),
                 )
 
-        def load_codes(w, half):
-            cols = slice(FEATURES // HALVES * half, FEATURES // HALVES * (half + 1))
+        def load_codes(w, half, first=0, last=FEATURES // HALVES):
+            cols = slice(FEATURES // HALVES * half + first, FEATURES // HALVES * half + last)
             nc.sync.dma_start(
-                out=w_codes[:, w, half, :, :],
+                out=w_codes[:, w, half, :, first:last],
                 in_=weight_words[w][:, :, cols, :].rearrange("g p n t -> p g (n t)").bitcast(I32),
+            )
+
+        def load_bias(w):
+            nc.sync.dma_start(
+                out=bias_rows[0:1, FEATURES * w : FEATURES * (w + 1)],
+                in_=biases[w].rearrange("(o n) -> o n", o=1),
             )
 
         x_rows = hidden_states.rearrange("b (u j) k -> u b (j k)", j=TOKEN_TILES)
@@ -103,13 +111,16 @@ def tile_attention_before_kernel(
         for i in range(len(X_PIECES)):
             piece = slice(HIDDEN * sum(X_PIECES[:i]), HIDDEN * sum(X_PIECES[: i + 1]))
             nc.sync.dma_start(out=x_flat[:, piece], in_=x_rows[:, :, piece])
-            if i == 0:
-                for w in range(WEIGHTS):
-                    nc.sync.dma_start(
-                        out=bias_rows[0:1, FEATURES * w : FEATURES * (w + 1)],
-                        in_=biases[w].rearrange("(o n) -> o n", o=1),
-                    )
-        for w in range(WEIGHTS):
+            if i == 1:
+                load_bias(0)
+            if i == 2:
+                load_bias(1)
+                load_bias(2)
+        load_codes(0, 0, 0, N_TILE)
+        load_scales(0)
+        load_codes(0, 0, N_TILE, FEATURES // HALVES)
+        load_codes(0, 1)
+        for w in range(1, WEIGHTS):
             load_codes(w, 0)
             load_scales(w)
             load_codes(w, 1)
@@ -135,8 +146,7 @@ def tile_attention_before_kernel(
                 scales=x_planes[:, j, :],
                 in_=x_grouped[:, j, :],
             )
-            if 1 <= j <= WEIGHTS * HALVES:
-                w, half = divmod(j - 1, HALVES)
+            for w, half in BIAS_SLOTS.get(j, []):
                 if half == 0:
                     bias_banks[w] = psum.tile([P, FEATURES], BF16, tag="bank", name="bias_bank%d" % w)
                 nc.tensor.matmul(

@@ -58,6 +58,7 @@ def tile_attention_before_kernel(
     with ExitStack() as ctx:
         keep = ctx.enter_context(tc.tile_pool(name="keep", bufs=1))
         psum = ctx.enter_context(tc.psum_pool(name="psum", bufs=8))
+        ctx.enter_context(tc.manual_schedule())
 
         x_sb = keep.tile([P, TOKEN_TILES, HIDDEN], BF16)
         x_grouped = keep.tile([P, TOKEN_TILES, PASSES * P * PACK], BF16, align_bytes=64)

from contextlib import ExitStack

import concourse.mybir as mybir
from concourse.masks import make_identity

BF16 = mybir.dt.bfloat16
F32 = mybir.dt.float32
I32 = mybir.dt.int32
U8 = mybir.dt.uint8
FP8X4 = mybir.dt.float8_e4m3fn_x4
ADD = mybir.AluOpType.add

P = 128
PACK = 4
K_PASS = P * PACK
BATCH, SEQ, HIDDEN = 2, 512, 1024
HEADS, HEAD_DIM = 16, 64
FEATURES = HEADS * HEAD_DIM
WEIGHTS = 3
PASSES = HIDDEN // K_PASS
TOKEN_TILES = BATCH * SEQ // P
BANK = 512
N_TILE = 256
COLUMN_TILES = [N_TILE] * (WEIGHTS * FEATURES // N_TILE - 1) + [N_TILE // 2] * 2
PAIRS = 2
HALVES = 2
X_PIECES = [1, 1, 2, 2, 2]
BIAS_SLOTS = {1: [(0, 0), (0, 1)], 3: [(1, 0)], 4: [(1, 1)], 5: [(2, 0)], 6: [(2, 1)]}
WARM_UP = 4
QUADRANTS = 4
SCALE_ROWS = 4

FLOPS = 2 * BATCH * SEQ * HIDDEN * WEIGHTS * FEATURES


def tile_attention_before_kernel(
    tc,
    hidden_states,
    Wq_words,
    Wq_scales,
    bq,
    Wk_words,
    Wk_scales,
    bk,
    Wv_words,
    Wv_scales,
    bv,
    out_0,
    out_1,
    out_2,
):
    nc = tc.nc
    weight_words = [Wq_words, Wk_words, Wv_words]
    weight_scales = [Wq_scales, Wk_scales, Wv_scales]
    biases = [bq, bk, bv]
    outs = [out_0, out_1, out_2]

    with ExitStack() as ctx:
        keep = ctx.enter_context(tc.tile_pool(name="keep", bufs=1))
        psum = ctx.enter_context(tc.psum_pool(name="psum", bufs=8))
        ctx.enter_context(tc.manual_schedule())

        x_sb = keep.tile([P, TOKEN_TILES, HIDDEN], BF16)
        x_grouped = keep.tile([P, TOKEN_TILES, PASSES * P * PACK], BF16, align_bytes=64)
        x_codes = keep.tile([P, TOKEN_TILES, PASSES * P], I32, align_bytes=64)
        x_planes = keep.tile([P, TOKEN_TILES, PASSES * P], U8, align_bytes=64)
        w_codes = keep.tile([P, WEIGHTS, HALVES, PASSES, FEATURES // HALVES], I32, align_bytes=64)
        w_planes = [
            keep.tile([P, PASSES, FEATURES], U8, align_bytes=64, name="w_planes%d" % w)
            for w in range(WEIGHTS)
        ]
        identity = keep.tile([P, P], F32)
        ones = keep.tile([P, BANK], BF16)
        bias_rows = keep.tile([P, WEIGHTS * FEATURES], BF16)
        bias_all = keep.tile([P, WEIGHTS * FEATURES], BF16)
        staged = keep.tile([P, WEIGHTS * HEADS, TOKEN_TILES, HEAD_DIM], F32)

        nc.vector.memset(ones[:], 1.0)
        for w in range(WEIGHTS):
            nc.vector.memset(bias_rows[:, FEATURES * w : FEATURES * (w + 1)].bitcast(I32), 0)
        for w in range(WEIGHTS):
            nc.vector.memset(w_planes[w][:].rearrange("p g n -> p (g n)").bitcast(I32), 0)
        make_identity(nc, identity[:])

        warm_bank = psum.tile([P, BANK], F32, tag="bank")
        for i in range(WARM_UP):
            nc.tensor.matmul(warm_bank[:], lhsT=ones[:, 0:P], rhs=ones[:], start=True, stop=True)

        def load_scales(w):
            rows = weight_scales[w].rearrange("g (q r) n -> r q g n", r=SCALE_ROWS)
            for r in range(SCALE_ROWS):
                nc.sync.dma_start(
                    out=w_planes[w][r : P : P // QUADRANTS, :, :].bitcast(I32),
                    in_=rows[r].bitcast(I32),
                )

        def load_codes(w, half, first=0, last=FEATURES // HALVES):
            cols = slice(FEATURES // HALVES * half + first, FEATURES // HALVES * half + last)
            nc.sync.dma_start(
                out=w_codes[:, w, half, :, first:last],
                in_=weight_words[w][:, :, cols, :].rearrange("g p n t -> p g (n t)").bitcast(I32),
            )

        def load_bias(w):
            nc.sync.dma_start(
                out=bias_rows[0:1, FEATURES * w : FEATURES * (w + 1)],
                in_=biases[w].rearrange("(o n) -> o n", o=1),
            )

        x_rows = hidden_states.rearrange("b (u j) k -> u b (j k)", j=TOKEN_TILES)
        x_flat = x_sb[:].rearrange("p j k -> p (j k)")
        for i in range(len(X_PIECES)):
            piece = slice(HIDDEN * sum(X_PIECES[:i]), HIDDEN * sum(X_PIECES[: i + 1]))
            nc.sync.dma_start(out=x_flat[:, piece], in_=x_rows[:, :, piece])
            if i == 1:
                load_bias(0)
            if i == 2:
                load_bias(1)
                load_bias(2)
        load_codes(0, 0, 0, N_TILE)
        load_scales(0)
        load_codes(0, 0, N_TILE, FEATURES // HALVES)
        load_codes(0, 1)
        for w in range(1, WEIGHTS):
            load_codes(w, 0)
            load_scales(w)
            load_codes(w, 1)

        words_per_pass = K_PASS // 2
        bias_banks = {}
        for j in range(TOKEN_TILES):
            x_words = x_sb[:, j, :].bitcast(F32)
            flipped = psum.tile([P, PASSES, PAIRS, P], F32, tag="bank")
            for g in range(PASSES):
                for e in range(PAIRS):
                    nc.tensor.transpose(
                        flipped[:, g, e, :],
                        x_words[:, words_per_pass * g + e : words_per_pass * (g + 1) : PAIRS],
                        identity[:],
                    )
            nc.scalar.copy(
                out=x_grouped[:, j, :].bitcast(F32).rearrange("p (g m e) -> p g m e", g=PASSES, e=PAIRS),
                in_=flipped[:].rearrange("p g e m -> p g m e"),
            )
            nc.vector.quantize_mx(
                out=x_codes[:, j, :].bitcast(FP8X4),
                scales=x_planes[:, j, :],
                in_=x_grouped[:, j, :],
            )
            for w, half in BIAS_SLOTS.get(j, []):
                if half == 0:
                    bias_banks[w] = psum.tile([P, FEATURES], BF16, tag="bank", name="bias_bank%d" % w)
                nc.tensor.matmul(
                    bias_banks[w][:, BANK * half : BANK * (half + 1)],
                    lhsT=ones[:, 0:P],
                    rhs=bias_rows[:, FEATURES * w + BANK * half : FEATURES * w + BANK * (half + 1)],
                    start=True,
                    stop=True,
                )
                if half == HALVES - 1:
                    nc.vector.tensor_copy(
                        out=bias_all[:, FEATURES * w : FEATURES * (w + 1)], in_=bias_banks[w][:]
                    )

        out_rows = [o.rearrange("b h (u j) d -> b u h (j d)", j=TOKEN_TILES) for o in outs]
        first = 0
        banks_done = 0
        for width in COLUMN_TILES:
            w = first // FEATURES
            in_weight = first % FEATURES
            half = in_weight // (FEATURES // HALVES)
            in_half = in_weight % (FEATURES // HALVES)
            heads_here = width // HEAD_DIM
            heads = slice(first // HEAD_DIM, first // HEAD_DIM + heads_here)
            per_bank = BANK // width
            bias_heads = (
                bias_all[:, first : first + width]
                .rearrange("p (i h d) -> p i h d", i=1, d=HEAD_DIM)
                .to_broadcast([P, per_bank, heads_here, HEAD_DIM])
            )
            for bank in range(TOKEN_TILES // per_bank):
                acc = psum.tile([P, per_bank, width], F32, tag="bank")
                for i in range(per_bank):
                    j = per_bank * bank + i
                    for g in range(PASSES):
                        tokens = slice(P * g, P * (g + 1))
                        nc.tensor.matmul_mx(
                            out=acc[:, i, :],
                            lhsT=x_codes[:, j, tokens].bitcast(FP8X4),
                            lhsT_scale=x_planes[:, j, tokens],
                            rhs=w_codes[:, w, half, g, in_half : in_half + width].bitcast(FP8X4),
                            rhs_scale=w_planes[w][:, g, in_weight : in_weight + width],
                            start=(g == 0),
                            stop=(g == PASSES - 1),
                        )
                acc_heads = acc[:].rearrange("p i (h d) -> p i h d", d=HEAD_DIM)
                token_tiles = slice(per_bank * bank, per_bank * (bank + 1))
                landing = staged[:, heads, token_tiles, :].rearrange("p h i d -> p i h d")
                if width == N_TILE and banks_done % 5 == 0:
                    nc.scalar.copy(out=landing, in_=acc_heads)
                    nc.gpsimd.tensor_tensor(out=landing, in0=landing, in1=bias_heads, op=ADD)
                else:
                    nc.vector.tensor_tensor(out=landing, in0=acc_heads, in1=bias_heads, op=ADD)
                banks_done += 1
            first_head = in_weight // HEAD_DIM
            for b in range(BATCH):
                nc.sync.dma_start(
                    out=out_rows[w][b][:, first_head : first_head + heads_here, :],
                    in_=staged[b:P:BATCH, heads, :, :].rearrange("p h j d -> p h (j d)"),
                )
            first += width
